import numpy as np
import ml_dtypes

BF16 = ml_dtypes.bfloat16


def bf(x):
    return np.asarray(x, np.float32).astype(BF16)


def f32(x):
    return np.asarray(x, np.float32)


def f64(x):
    return np.asarray(x).astype(np.float64)


def striped(idx):
    return np.tile(idx.reshape(-1, 16).T, (8, 1))


C, S, B, BAG, P, L1, L2, M, N, H = 512, 2048, 512, 8, 2, 2048, 1024, 128, 8192, 1024


def crelu(v):
    return np.minimum(np.maximum(v, 0.0), 1.0)


def setup_inputs():
    return {
        "emb": f32(0.25 * np.random.standard_normal((C, S))),
        "w1": bf(0.05 * np.random.standard_normal((P * C, L1))),
        "b1": f32(0.1 * np.random.standard_normal((L1, 1))),
        "w2": bf(0.035 * np.random.standard_normal((L1, L2))),
        "b2": f32(0.1 * np.random.standard_normal((L2, 1))),
        "w3": bf(0.05 * np.random.standard_normal((L2, M))),
        "b3": f32(0.1 * np.random.standard_normal((M, 1))),
        "offs": striped(np.concatenate([np.random.permutation(S)[:H] for _ in range(BAG)])),
    }


def reference(emb, w1, b1, w2, b2, w3, b3, offs):
    idx = offs[:16].T.reshape(-1)
    acc = f64(emb)[:, idx].reshape(C, BAG, P, B).sum(axis=1)
    x = crelu(acc.transpose(1, 0, 2).reshape(P * C, B))
    h1 = crelu(f64(w1).T @ x + f64(b1))
    h2 = crelu(f64(w2).T @ h1 + f64(b2))
    return f64(w3).T @ h2 + f64(b3)

@@ -1,0 +1,140 @@
+import concourse.mybir as mybir
+
+F32 = mybir.dt.float32
+BF16 = mybir.dt.bfloat16
+U16 = mybir.dt.uint16
+ADD = mybir.AluOpType.add
+RELU = mybir.ActivationFunctionType.Relu
+IDENTITY = mybir.ActivationFunctionType.Identity
+
+P = 128
+C, S, B, BAG, SIDES = 512, 2048, 512, 8, 2
+L1, L2, M = 2048, 1024, 128
+N = BAG * SIDES * B
+
+CB = C // P
+XB = SIDES * CB
+H1B = L1 // P
+H2B = L2 // P
+
+T = 128
+BANK = 512
+IN_BANK = BANK // T
+
+FLOPS = 2 * B * (SIDES * C * L1 + L1 * L2 + L2 * M)
+
+
+def tile_nnue_b_kernel(tc, emb, w1, b1, w2, b2, w3, b3, offs, out):
+    nc = tc.nc
+    with (
+        tc.tile_pool(name="held", bufs=1) as held,
+        tc.tile_pool(name="sums", bufs=3 * BAG) as sums,
+        tc.tile_pool(name="work", bufs=3) as work,
+        tc.tile_pool(name="xs", bufs=2 * CB) as xs,
+        tc.tile_pool(name="acts", bufs=2) as acts,
+        tc.psum_pool(name="banks1", bufs=H1B // IN_BANK + 1) as banks1,
+        tc.psum_pool(name="banks2", bufs=H2B // IN_BANK) as banks2,
+        tc.psum_pool(name="banks3", bufs=1) as banks3,
+    ):
+        offsets = held.tile([P, N // 16], U16, name="offsets")
+        nc.sync.dma_start(offsets[:], offs)
+
+        emb_t = [held.tile([P, S], F32, name=f"emb{cb}") for cb in range(CB)]
+        w1_t = [held.tile([P, L1], BF16, name=f"w1_{kb}") for kb in range(XB)]
+        w2_t = [held.tile([P, L2], BF16, name=f"w2_{kb}") for kb in range(H1B)]
+        w3_t = held.tile([P, H2B * M], BF16, name="w3_t")
+        b1_t = held.tile([P, H1B], F32, name="b1_t")
+        b2_t = held.tile([P, H2B], F32, name="b2_t")
+        b3_t = held.tile([P, 1], F32, name="b3_t")
+
+        loads = []
+        for cb in range(CB):
+            loads.append((emb_t[cb][:], emb[cb * P : (cb + 1) * P, :]))
+            for s in range(SIDES):
+                kb = s * CB + cb
+                loads.append((w1_t[kb][:], w1[kb * P : (kb + 1) * P, :]))
+        loads.append((b1_t[:], b1.rearrange("(a p) o -> p (a o)", p=P)))
+        for kb in range(H1B):
+            loads.append((w2_t[kb][:], w2[kb * P : (kb + 1) * P, :]))
+        loads.append((b2_t[:], b2.rearrange("(a p) o -> p (a o)", p=P)))
+        loads.append((w3_t[:].rearrange("p (a m) -> p a m", m=M), w3.rearrange("(a p) m -> p a m", p=P)))
+        loads.append((b3_t[:], b3))
+        for n, (tile_ap, dram_ap) in enumerate(loads):
+            queue = nc.scalar if n % 2 == 0 else nc.sync
+            queue.dma_start(tile_ap, dram_ap)
+
+        zeros = held.tile([P, SIDES * T], F32, name="zeros")
+        nc.vector.memset(zeros[:], 0.0)
+        one = held.tile([P, 1], F32, name="one")
+        nc.vector.memset(one[:], 1.0)
+
+        def flip(out_ap, in_ap, bias_ap):
+            nc.scalar.activation(out_ap, in_ap, RELU, bias=bias_ap, scale=-1.0)
+
+        one_less_b1 = held.tile([P, H1B], F32, name="one_less_b1")
+        nc.scalar.activation(one_less_b1[:], b1_t[:], IDENTITY, bias=one[:], scale=-1.0)
+        one_less_b2 = held.tile([P, H2B], F32, name="one_less_b2")
+        nc.scalar.activation(one_less_b2[:], b2_t[:], IDENTITY, bias=one[:], scale=-1.0)
+
+        def product(banks, weights, kb, last_kb, moving):
+            for mb in range(len(banks) * IN_BANK):
+                place = mb % IN_BANK
+                nc.tensor.matmul(
+                    banks[mb // IN_BANK][:, place * T : (place + 1) * T],
+                    weights[:, mb * P : (mb + 1) * P],
+                    moving,
+                    start=(kb == 0 and place == 0),
+                    stop=(kb == last_kb and place == IN_BANK - 1),
+                )
+
+        def clip(hidden, banks, one_less_b):
+            for g, bank in enumerate(banks):
+                flipped = work.tile([P, BANK], F32, name="flipped")
+                for place in range(IN_BANK):
+                    mb = g * IN_BANK + place
+                    cols = slice(place * T, (place + 1) * T)
+                    flip(flipped[:, cols], bank[:, cols], one_less_b[:, mb : mb + 1])
+                flip(hidden[:, g * BANK : (g + 1) * BANK], flipped[:], one[:])
+
+        for t0 in range(0, B, T):
+            h1_banks = [banks1.tile([P, BANK], F32, name="h1_bank") for g in range(H1B // IN_BANK)]
+            for cb in range(CB):
+                total = zeros
+                for k in range(BAG):
+                    longer = sums.tile([P, SIDES * T], F32, name="longer")
+                    for s in range(SIDES):
+                        first = (k * SIDES * B + s * B + t0) // 16
+                        nc.vector.tensor_tensor(
+                            longer[:, s * T : (s + 1) * T],
+                            emb_t[cb][:].indirect(offsets[:, first : first + T // 16]),
+                            total[:, s * T : (s + 1) * T],
+                            ADD,
+                        )
+                    total = longer
+                x_flipped = work.tile([P, SIDES * T], F32, name="x_flipped")
+                flip(x_flipped[:], total[:], one[:])
+                x = xs.tile([P, SIDES * T], BF16, name="x")
+                flip(x[:], x_flipped[:], one[:])
+                for s in range(SIDES):
+                    product(h1_banks, w1_t[s * CB + cb], SIDES * cb + s, XB - 1, x[:, s * T : (s + 1) * T])
+            h1 = acts.tile([P, H1B * T], BF16, name="h1")
+            clip(h1, h1_banks, one_less_b1)
+
+            h2_banks = [banks2.tile([P, BANK], F32, name="h2_bank") for g in range(H2B // IN_BANK)]
+            for kb in range(H1B):
+                product(h2_banks, w2_t[kb], kb, H1B - 1, h1[:, kb * T : (kb + 1) * T])
+            h2 = acts.tile([P, H2B * T], BF16, name="h2")
+            clip(h2, h2_banks, one_less_b2)
+
+            out_bank = banks3.tile([P, T], F32, name="out_bank")
+            for kb in range(H2B):
+                nc.tensor.matmul(
+                    out_bank[:],
+                    w3_t[:, kb * M : (kb + 1) * M],
+                    h2[:, kb * T : (kb + 1) * T],
+                    start=(kb == 0),
+                    stop=(kb == H2B - 1),
+                )
+            result = work.tile([P, T], F32, name="result")
+            nc.scalar.activation(result[:], out_bank[:], IDENTITY, bias=b3_t[:], scale=1.0)
+            nc.sync.dma_start(out[:, t0 : t0 + T], result[:])

@@ -4,6 +4,8 @@ F32 = mybir.dt.float32
 BF16 = mybir.dt.bfloat16
 U16 = mybir.dt.uint16
 ADD = mybir.AluOpType.add
+MAX = mybir.AluOpType.max
+MIN = mybir.AluOpType.min
 RELU = mybir.ActivationFunctionType.Relu
 IDENTITY = mybir.ActivationFunctionType.Identity
 
@@ -16,10 +18,12 @@ CB = C // P
 XB = SIDES * CB
 H1B = L1 // P
 H2B = L2 // P
+QUARTER = H1B // CB
 
-T = 128
+CHUNKS = (128, 128, 128, 64, 64)
+WIDEST = max(CHUNKS)
 BANK = 512
-IN_BANK = BANK // T
+HALF = BAG // 2
 
 FLOPS = 2 * B * (SIDES * C * L1 + L1 * L2 + L2 * M)
 
@@ -32,8 +36,8 @@ def tile_nnue_b_kernel(tc, emb, w1, b1, w2, b2, w3, b3, offs, out):
         tc.tile_pool(name="work", bufs=3) as work,
         tc.tile_pool(name="xs", bufs=2 * CB) as xs,
         tc.tile_pool(name="acts", bufs=2) as acts,
-        tc.psum_pool(name="banks1", bufs=H1B // IN_BANK + 1) as banks1,
-        tc.psum_pool(name="banks2", bufs=H2B // IN_BANK) as banks2,
+        tc.psum_pool(name="banks1", bufs=H1B * WIDEST // BANK + 1) as banks1,
+        tc.psum_pool(name="banks2", bufs=H2B * WIDEST // BANK) as banks2,
         tc.psum_pool(name="banks3", bufs=1) as banks3,
     ):
         offsets = held.tile([P, N // 16], U16, name="offsets")
@@ -47,23 +51,25 @@ def tile_nnue_b_kernel(tc, emb, w1, b1, w2, b2, w3, b3, offs, out):
         b2_t = held.tile([P, H2B], F32, name="b2_t")
         b3_t = held.tile([P, 1], F32, name="b3_t")
 
-        loads = []
+        def load_emb(cb):
+            nc.sync.dma_start(emb_t[cb][:], emb[cb * P : (cb + 1) * P, :])
+
+        load_emb(0)
+        load_emb(1)
+        nc.sync.dma_start(b1_t[:], b1.rearrange("(a p) o -> p (a o)", p=P))
+        nc.sync.dma_start(b2_t[:], b2.rearrange("(a p) o -> p (a o)", p=P))
+        nc.sync.dma_start(b3_t[:], b3)
         for cb in range(CB):
-            loads.append((emb_t[cb][:], emb[cb * P : (cb + 1) * P, :]))
             for s in range(SIDES):
                 kb = s * CB + cb
-                loads.append((w1_t[kb][:], w1[kb * P : (kb + 1) * P, :]))
-        loads.append((b1_t[:], b1.rearrange("(a p) o -> p (a o)", p=P)))
+                nc.sync.dma_start(w1_t[kb][:], w1[kb * P : (kb + 1) * P, :])
+            if cb + 2 < CB:
+                load_emb(cb + 2)
         for kb in range(H1B):
-            loads.append((w2_t[kb][:], w2[kb * P : (kb + 1) * P, :]))
-        loads.append((b2_t[:], b2.rearrange("(a p) o -> p (a o)", p=P)))
-        loads.append((w3_t[:].rearrange("p (a m) -> p a m", m=M), w3.rearrange("(a p) m -> p a m", p=P)))
-        loads.append((b3_t[:], b3))
-        for n, (tile_ap, dram_ap) in enumerate(loads):
-            queue = nc.scalar if n % 2 == 0 else nc.sync
-            queue.dma_start(tile_ap, dram_ap)
+            nc.sync.dma_start(w2_t[kb][:], w2[kb * P : (kb + 1) * P, :])
+        nc.sync.dma_start(w3_t[:].rearrange("p (a m) -> p a m", m=M), w3.rearrange("(a p) m -> p a m", p=P))
 
-        zeros = held.tile([P, SIDES * T], F32, name="zeros")
+        zeros = held.tile([P, SIDES * WIDEST], F32, name="zeros")
         nc.vector.memset(zeros[:], 0.0)
         one = held.tile([P, 1], F32, name="one")
         nc.vector.memset(one[:], 1.0)
@@ -76,65 +82,104 @@ def tile_nnue_b_kernel(tc, emb, w1, b1, w2, b2, w3, b3, offs, out):
         one_less_b2 = held.tile([P, H2B], F32, name="one_less_b2")
         nc.scalar.activation(one_less_b2[:], b2_t[:], IDENTITY, bias=one[:], scale=-1.0)
 
-        def product(banks, weights, kb, last_kb, moving):
-            for mb in range(len(banks) * IN_BANK):
-                place = mb % IN_BANK
-                nc.tensor.matmul(
-                    banks[mb // IN_BANK][:, place * T : (place + 1) * T],
-                    weights[:, mb * P : (mb + 1) * P],
-                    moving,
-                    start=(kb == 0 and place == 0),
-                    stop=(kb == last_kb and place == IN_BANK - 1),
+        def add_slot(total, t0, width, cb, k):
+            longer = sums.tile([P, SIDES * width], F32, name="longer")
+            for s in range(SIDES):
+                first = (k * SIDES * B + s * B + t0) // 16
+                nc.vector.tensor_tensor(
+                    longer[:, s * width : (s + 1) * width],
+                    emb_t[cb][:].indirect(offsets[:, first : first + width // 16]),
+                    total[:, s * width : (s + 1) * width],
+                    ADD,
                 )
+            return longer
 
-        def clip(hidden, banks, one_less_b):
+        def open_banks(pool, blocks, width, name):
+            return [pool.tile([P, BANK], F32, name=name) for g in range(blocks * width // BANK)]
+
+        def product(banks, width, shares, last):
+            in_bank = BANK // width
+            for g, bank in enumerate(banks):
+                for number, weights, moving in shares:
+                    for place in range(in_bank):
+                        mb = g * in_bank + place
+                        nc.tensor.matmul(
+                            bank[:, place * width : (place + 1) * width],
+                            weights[:, mb * P : (mb + 1) * P],
+                            moving,
+                            start=(number == 0 and place == 0),
+                            stop=(number == last and place == in_bank - 1),
+                        )
+
+        def clip(hidden, banks, width, one_less_b):
+            in_bank = BANK // width
             for g, bank in enumerate(banks):
                 flipped = work.tile([P, BANK], F32, name="flipped")
-                for place in range(IN_BANK):
-                    mb = g * IN_BANK + place
-                    cols = slice(place * T, (place + 1) * T)
+                for place in range(in_bank):
+                    mb = g * in_bank + place
+                    cols = slice(place * width, (place + 1) * width)
                     flip(flipped[:, cols], bank[:, cols], one_less_b[:, mb : mb + 1])
                 flip(hidden[:, g * BANK : (g + 1) * BANK], flipped[:], one[:])
 
-        for t0 in range(0, B, T):
-            h1_banks = [banks1.tile([P, BANK], F32, name="h1_bank") for g in range(H1B // IN_BANK)]
-            for cb in range(CB):
-                total = zeros
-                for k in range(BAG):
-                    longer = sums.tile([P, SIDES * T], F32, name="longer")
-                    for s in range(SIDES):
-                        first = (k * SIDES * B + s * B + t0) // 16
-                        nc.vector.tensor_tensor(
-                            longer[:, s * T : (s + 1) * T],
-                            emb_t[cb][:].indirect(offsets[:, first : first + T // 16]),
-                            total[:, s * T : (s + 1) * T],
-                            ADD,
-                        )
-                    total = longer
-                x_flipped = work.tile([P, SIDES * T], F32, name="x_flipped")
-                flip(x_flipped[:], total[:], one[:])
-                x = xs.tile([P, SIDES * T], BF16, name="x")
-                flip(x[:], x_flipped[:], one[:])
-                for s in range(SIDES):
-                    product(h1_banks, w1_t[s * CB + cb], SIDES * cb + s, XB - 1, x[:, s * T : (s + 1) * T])
-            h1 = acts.tile([P, H1B * T], BF16, name="h1")
-            clip(h1, h1_banks, one_less_b1)
-
-            h2_banks = [banks2.tile([P, BANK], F32, name="h2_bank") for g in range(H2B // IN_BANK)]
-            for kb in range(H1B):
-                product(h2_banks, w2_t[kb], kb, H1B - 1, h1[:, kb * T : (kb + 1) * T])
-            h2 = acts.tile([P, H2B * T], BF16, name="h2")
-            clip(h2, h2_banks, one_less_b2)
-
-            out_bank = banks3.tile([P, T], F32, name="out_bank")
+        def layer3(t0, width, h2):
+            out_bank = banks3.tile([P, width], F32, name="out_bank")
             for kb in range(H2B):
                 nc.tensor.matmul(
                     out_bank[:],
                     w3_t[:, kb * M : (kb + 1) * M],
-                    h2[:, kb * T : (kb + 1) * T],
+                    h2[:, kb * width : (kb + 1) * width],
                     start=(kb == 0),
                     stop=(kb == H2B - 1),
                 )
-            result = work.tile([P, T], F32, name="result")
+            result = work.tile([P, width], F32, name="result")
             nc.scalar.activation(result[:], out_bank[:], IDENTITY, bias=b3_t[:], scale=1.0)
-            nc.sync.dma_start(out[:, t0 : t0 + T], result[:])
+            nc.sync.dma_start(out[:, t0 : t0 + width], result[:])
+
+        steps = [(r, cb) for r in range(len(CHUNKS)) for cb in range(CB)]
+        starts = [sum(CHUNKS[:r]) for r in range(len(CHUNKS))]
+        totals = {}
+        h1_banks, h2_banks, h1, h2 = {}, {}, {}, {}
+
+        def follow(r, quarter):
+            width = CHUNKS[r]
+            if quarter == 0:
+                h2_banks[r] = open_banks(banks2, H2B, width, "h2_bank")
+            shares = [
+                (kb, w2_t[kb], h1[r][:, kb * width : (kb + 1) * width])
+                for kb in range(quarter * QUARTER, (quarter + 1) * QUARTER)
+            ]
+            product(h2_banks[r], width, shares, H1B - 1)
+            if quarter == CB - 1:
+                h2[r] = acts.tile([P, H2B * width], BF16, name="h2")
+                clip(h2[r], h2_banks[r], width, one_less_b2)
+            if quarter == 0 and r > 0:
+                layer3(starts[r - 1], CHUNKS[r - 1], h2[r - 1])
+
+        def finish_step(r, cb):
+            width = CHUNKS[r]
+            x = xs.tile([P, SIDES * width], BF16, name="x")
+            nc.vector.tensor_scalar(x[:], totals[(r, cb)][:], 0.0, 1.0, op0=MAX, op1=MIN)
+            if cb == 0:
+                h1_banks[r] = open_banks(banks1, H1B, width, "h1_bank")
+            shares = [(SIDES * cb + s, w1_t[s * CB + cb], x[:, s * width : (s + 1) * width]) for s in range(SIDES)]
+            product(h1_banks[r], width, shares, XB - 1)
+            if cb == CB - 1:
+                h1[r] = acts.tile([P, H1B * width], BF16, name="h1")
+                clip(h1[r], h1_banks[r], width, one_less_b1)
+            if r > 0:
+                follow(r - 1, cb)
+
+        for n in range(len(steps) + 1):
+            for i in range(HALF):
+                if n > 0:
+                    r, cb = steps[n - 1]
+                    totals[(r, cb)] = add_slot(totals[(r, cb)], starts[r], CHUNKS[r], cb, HALF + i)
+                if n < len(steps):
+                    r, cb = steps[n]
+                    totals[(r, cb)] = add_slot(totals.get((r, cb), zeros), starts[r], CHUNKS[r], cb, i)
+            if n > 0:
+                finish_step(*steps[n - 1])
+        last = len(CHUNKS) - 1
+        for quarter in range(CB):
+            follow(last, quarter)
+        layer3(starts[last], CHUNKS[last], h2[last])

@@ -18,12 +18,11 @@ CB = C // P
 XB = SIDES * CB
 H1B = L1 // P
 H2B = L2 // P
-QUARTER = H1B // CB
+PER_STEP = H1B // 2
 
-CHUNKS = (128, 128, 128, 64, 64)
+CHUNKS = (128, 128, 128, 128)
 WIDEST = max(CHUNKS)
 BANK = 512
-HALF = BAG // 2
 
 FLOPS = 2 * B * (SIDES * C * L1 + L1 * L2 + L2 * M)
 
@@ -140,20 +139,21 @@ def tile_nnue_b_kernel(tc, emb, w1, b1, w2, b2, w3, b3, offs, out):
         totals = {}
         h1_banks, h2_banks, h1, h2 = {}, {}, {}, {}
 
-        def follow(r, quarter):
+        def follow(r, part):
             width = CHUNKS[r]
-            if quarter == 0:
+            if part == 2:
+                layer3(starts[r], width, h2[r])
+                return
+            if part == 0:
                 h2_banks[r] = open_banks(banks2, H2B, width, "h2_bank")
             shares = [
                 (kb, w2_t[kb], h1[r][:, kb * width : (kb + 1) * width])
-                for kb in range(quarter * QUARTER, (quarter + 1) * QUARTER)
+                for kb in range(part * PER_STEP, (part + 1) * PER_STEP)
             ]
             product(h2_banks[r], width, shares, H1B - 1)
-            if quarter == CB - 1:
+            if part == 1:
                 h2[r] = acts.tile([P, H2B * width], BF16, name="h2")
                 clip(h2[r], h2_banks[r], width, one_less_b2)
-            if quarter == 0 and r > 0:
-                layer3(starts[r - 1], CHUNKS[r - 1], h2[r - 1])
 
         def finish_step(r, cb):
             width = CHUNKS[r]
@@ -166,20 +166,15 @@ def tile_nnue_b_kernel(tc, emb, w1, b1, w2, b2, w3, b3, offs, out):
             if cb == CB - 1:
                 h1[r] = acts.tile([P, H1B * width], BF16, name="h1")
                 clip(h1[r], h1_banks[r], width, one_less_b1)
-            if r > 0:
+            if r > 0 and cb < 3:
                 follow(r - 1, cb)
 
-        for n in range(len(steps) + 1):
-            for i in range(HALF):
-                if n > 0:
-                    r, cb = steps[n - 1]
-                    totals[(r, cb)] = add_slot(totals[(r, cb)], starts[r], CHUNKS[r], cb, HALF + i)
-                if n < len(steps):
-                    r, cb = steps[n]
-                    totals[(r, cb)] = add_slot(totals.get((r, cb), zeros), starts[r], CHUNKS[r], cb, i)
-            if n > 0:
-                finish_step(*steps[n - 1])
-        last = len(CHUNKS) - 1
-        for quarter in range(CB):
-            follow(last, quarter)
-        layer3(starts[last], CHUNKS[last], h2[last])
+        for n, (r, cb) in enumerate(steps):
+            totals[(r, cb)] = zeros
+            for k in range(BAG):
+                totals[(r, cb)] = add_slot(totals[(r, cb)], starts[r], CHUNKS[r], cb, k)
+                if k == 0 and n > 0:
+                    finish_step(*steps[n - 1])
+        finish_step(*steps[-1])
+        for part in range(3):
+            follow(len(CHUNKS) - 1, part)

@@ -4,8 +4,6 @@ F32 = mybir.dt.float32
 BF16 = mybir.dt.bfloat16
 U16 = mybir.dt.uint16
 ADD = mybir.AluOpType.add
-MAX = mybir.AluOpType.max
-MIN = mybir.AluOpType.min
 RELU = mybir.ActivationFunctionType.Relu
 IDENTITY = mybir.ActivationFunctionType.Identity
 
@@ -32,7 +30,7 @@ def tile_nnue_b_kernel(tc, emb, w1, b1, w2, b2, w3, b3, offs, out):
     with (
         tc.tile_pool(name="held", bufs=1) as held,
         tc.tile_pool(name="sums", bufs=3 * BAG) as sums,
-        tc.tile_pool(name="work", bufs=3) as work,
+        tc.tile_pool(name="work", bufs=2) as work,
         tc.tile_pool(name="xs", bufs=2 * CB) as xs,
         tc.tile_pool(name="acts", bufs=2) as acts,
         tc.psum_pool(name="banks1", bufs=H1B * WIDEST // BANK + 1) as banks1,
@@ -142,6 +140,8 @@ def tile_nnue_b_kernel(tc, emb, w1, b1, w2, b2, w3, b3, offs, out):
         def follow(r, part):
             width = CHUNKS[r]
             if part == 2:
+                h2[r] = acts.tile([P, H2B * width], BF16, name="h2")
+                clip(h2[r], h2_banks[r], width, one_less_b2)
                 layer3(starts[r], width, h2[r])
                 return
             if part == 0:
@@ -151,14 +151,13 @@ def tile_nnue_b_kernel(tc, emb, w1, b1, w2, b2, w3, b3, offs, out):
                 for kb in range(part * PER_STEP, (part + 1) * PER_STEP)
             ]
             product(h2_banks[r], width, shares, H1B - 1)
-            if part == 1:
-                h2[r] = acts.tile([P, H2B * width], BF16, name="h2")
-                clip(h2[r], h2_banks[r], width, one_less_b2)
 
         def finish_step(r, cb):
             width = CHUNKS[r]
             x = xs.tile([P, SIDES * width], BF16, name="x")
-            nc.vector.tensor_scalar(x[:], totals[(r, cb)][:], 0.0, 1.0, op0=MAX, op1=MIN)
+            flipped = work.tile([P, BANK], F32, name="flipped")
+            flip(flipped[:, : SIDES * width], totals[(r, cb)][:], one[:])
+            flip(x[:], flipped[:, : SIDES * width], one[:])
             if cb == 0:
                 h1_banks[r] = open_banks(banks1, H1B, width, "h1_bank")
             shares = [(SIDES * cb + s, w1_t[s * CB + cb], x[:, s * width : (s + 1) * width]) for s in range(SIDES)]
@@ -166,8 +165,9 @@ def tile_nnue_b_kernel(tc, emb, w1, b1, w2, b2, w3, b3, offs, out):
             if cb == CB - 1:
                 h1[r] = acts.tile([P, H1B * width], BF16, name="h1")
                 clip(h1[r], h1_banks[r], width, one_less_b1)
-            if r > 0 and cb < 3:
-                follow(r - 1, cb)
+                follow(r, 0)
+            if r > 0 and cb < 2:
+                follow(r - 1, cb + 1)
 
         for n, (r, cb) in enumerate(steps):
             totals[(r, cb)] = zeros
@@ -176,5 +176,5 @@ def tile_nnue_b_kernel(tc, emb, w1, b1, w2, b2, w3, b3, offs, out):
                 if k == 0 and n > 0:
                     finish_step(*steps[n - 1])
         finish_step(*steps[-1])
-        for part in range(3):
+        for part in (1, 2):
             follow(len(CHUNKS) - 1, part)

@@ -4,6 +4,8 @@ F32 = mybir.dt.float32
 BF16 = mybir.dt.bfloat16
 U16 = mybir.dt.uint16
 ADD = mybir.AluOpType.add
+MAX = mybir.AluOpType.max
+MIN = mybir.AluOpType.min
 RELU = mybir.ActivationFunctionType.Relu
 IDENTITY = mybir.ActivationFunctionType.Identity
 
@@ -30,7 +32,7 @@ def tile_nnue_b_kernel(tc, emb, w1, b1, w2, b2, w3, b3, offs, out):
     with (
         tc.tile_pool(name="held", bufs=1) as held,
         tc.tile_pool(name="sums", bufs=3 * BAG) as sums,
-        tc.tile_pool(name="work", bufs=2) as work,
+        tc.tile_pool(name="work", bufs=1) as work,
         tc.tile_pool(name="xs", bufs=2 * CB) as xs,
         tc.tile_pool(name="acts", bufs=2) as acts,
         tc.psum_pool(name="banks1", bufs=H1B * WIDEST // BANK + 1) as banks1,
@@ -155,9 +157,12 @@ def tile_nnue_b_kernel(tc, emb, w1, b1, w2, b2, w3, b3, offs, out):
         def finish_step(r, cb):
             width = CHUNKS[r]
             x = xs.tile([P, SIDES * width], BF16, name="x")
-            flipped = work.tile([P, BANK], F32, name="flipped")
-            flip(flipped[:, : SIDES * width], totals[(r, cb)][:], one[:])
-            flip(x[:], flipped[:, : SIDES * width], one[:])
+            if (r, cb) != steps[-1]:
+                flipped = work.tile([P, BANK], F32, name="flipped")
+                flip(flipped[:, : SIDES * width], totals[(r, cb)][:], one[:])
+                flip(x[:], flipped[:, : SIDES * width], one[:])
+            else:
+                nc.vector.tensor_scalar(x[:], totals[(r, cb)][:], 0.0, 1.0, op0=MAX, op1=MIN)
             if cb == 0:
                 h1_banks[r] = open_banks(banks1, H1B, width, "h1_bank")
             shares = [(SIDES * cb + s, w1_t[s * CB + cb], x[:, s * width : (s + 1) * width]) for s in range(SIDES)]

@@ -23,6 +23,8 @@ PER_STEP = H1B // 2
 CHUNKS = (128, 128, 128, 128)
 WIDEST = max(CHUNKS)
 BANK = 512
+H1_BANKS = 4
+H2_BANKS = 4
 
 FLOPS = 2 * B * (SIDES * C * L1 + L1 * L2 + L2 * M)
 
@@ -35,9 +37,8 @@ def tile_nnue_b_kernel(tc, emb, w1, b1, w2, b2, w3, b3, offs, out):
         tc.tile_pool(name="work", bufs=1) as work,
         tc.tile_pool(name="xs", bufs=2 * CB) as xs,
         tc.tile_pool(name="acts", bufs=2) as acts,
-        tc.psum_pool(name="banks1", bufs=H1B * WIDEST // BANK + 1) as banks1,
-        tc.psum_pool(name="banks2", bufs=H2B * WIDEST // BANK) as banks2,
-        tc.psum_pool(name="banks3", bufs=1) as banks3,
+        tc.psum_pool(name="banks1", bufs=H1_BANKS) as banks1,
+        tc.psum_pool(name="banks2", bufs=H2_BANKS) as banks2,
     ):
         offsets = held.tile([P, N // 16], U16, name="offsets")
         nc.sync.dma_start(offsets[:], offs)
@@ -93,11 +94,11 @@ def tile_nnue_b_kernel(tc, emb, w1, b1, w2, b2, w3, b3, offs, out):
                 )
             return longer
 
-        def open_banks(pool, blocks, width, name):
-            return [pool.tile([P, BANK], F32, name=name) for g in range(blocks * width // BANK)]
+        def open_banks(pool, count, name):
+            return [pool.tile([P, BANK], F32, name=name) for g in range(count)]
 
-        def product(banks, width, shares, last):
-            in_bank = BANK // width
+        def product(banks, blocks, width, shares, last):
+            in_bank = blocks // len(banks)
             for g, bank in enumerate(banks):
                 for number, weights, moving in shares:
                     for place in range(in_bank):
@@ -110,28 +111,28 @@ def tile_nnue_b_kernel(tc, emb, w1, b1, w2, b2, w3, b3, offs, out):
                             stop=(number == last and place == in_bank - 1),
                         )
 
-        def clip(hidden, banks, width, one_less_b):
-            in_bank = BANK // width
+        def clip(hidden, banks, blocks, width, one_less_b):
+            in_bank = blocks // len(banks)
+            used = in_bank * width
             for g, bank in enumerate(banks):
                 flipped = work.tile([P, BANK], F32, name="flipped")
                 for place in range(in_bank):
                     mb = g * in_bank + place
                     cols = slice(place * width, (place + 1) * width)
                     flip(flipped[:, cols], bank[:, cols], one_less_b[:, mb : mb + 1])
-                flip(hidden[:, g * BANK : (g + 1) * BANK], flipped[:], one[:])
+                flip(hidden[:, g * used : (g + 1) * used], flipped[:, :used], one[:])
 
-        def layer3(t0, width, h2):
-            out_bank = banks3.tile([P, width], F32, name="out_bank")
+        def layer3(t0, width, h2, out_bank):
             for kb in range(H2B):
                 nc.tensor.matmul(
-                    out_bank[:],
+                    out_bank,
                     w3_t[:, kb * M : (kb + 1) * M],
                     h2[:, kb * width : (kb + 1) * width],
                     start=(kb == 0),
                     stop=(kb == H2B - 1),
                 )
             result = work.tile([P, width], F32, name="result")
-            nc.scalar.activation(result[:], out_bank[:], IDENTITY, bias=b3_t[:], scale=1.0)
+            nc.scalar.activation(result[:], out_bank, IDENTITY, bias=b3_t[:], scale=1.0)
             nc.sync.dma_start(out[:, t0 : t0 + width], result[:])
 
         steps = [(r, cb) for r in range(len(CHUNKS)) for cb in range(CB)]
@@ -143,16 +144,16 @@ def tile_nnue_b_kernel(tc, emb, w1, b1, w2, b2, w3, b3, offs, out):
             width = CHUNKS[r]
             if part == 2:
                 h2[r] = acts.tile([P, H2B * width], BF16, name="h2")
-                clip(h2[r], h2_banks[r], width, one_less_b2)
-                layer3(starts[r], width, h2[r])
+                clip(h2[r], h2_banks[r], H2B, width, one_less_b2)
+                layer3(starts[r], width, h2[r], h2_banks[r][-1][:, BANK - width :])
                 return
             if part == 0:
-                h2_banks[r] = open_banks(banks2, H2B, width, "h2_bank")
+                h2_banks[r] = open_banks(banks2, H2_BANKS, "h2_bank")
             shares = [
                 (kb, w2_t[kb], h1[r][:, kb * width : (kb + 1) * width])
                 for kb in range(part * PER_STEP, (part + 1) * PER_STEP)
             ]
-            product(h2_banks[r], width, shares, H1B - 1)
+            product(h2_banks[r], H2B, width, shares, H1B - 1)
 
         def finish_step(r, cb):
             width = CHUNKS[r]
@@ -164,12 +165,12 @@ def tile_nnue_b_kernel(tc, emb, w1, b1, w2, b2, w3, b3, offs, out):
             else:
                 nc.vector.tensor_scalar(x[:], totals[(r, cb)][:], 0.0, 1.0, op0=MAX, op1=MIN)
             if cb == 0:
-                h1_banks[r] = open_banks(banks1, H1B, width, "h1_bank")
+                h1_banks[r] = open_banks(banks1, H1_BANKS, "h1_bank")
             shares = [(SIDES * cb + s, w1_t[s * CB + cb], x[:, s * width : (s + 1) * width]) for s in range(SIDES)]
-            product(h1_banks[r], width, shares, XB - 1)
+            product(h1_banks[r], H1B, width, shares, XB - 1)
             if cb == CB - 1:
                 h1[r] = acts.tile([P, H1B * width], BF16, name="h1")
-                clip(h1[r], h1_banks[r], width, one_less_b1)
+                clip(h1[r], h1_banks[r], H1B, width, one_less_b1)
                 follow(r, 0)
             if r > 0 and cb < 2:
                 follow(r - 1, cb + 1)

@@ -163,7 +163,9 @@ def tile_nnue_b_kernel(tc, emb, w1, b1, w2, b2, w3, b3, offs, out):
                 flip(flipped[:, : SIDES * width], totals[(r, cb)][:], one[:])
                 flip(x[:], flipped[:, : SIDES * width], one[:])
             else:
-                nc.vector.tensor_scalar(x[:], totals[(r, cb)][:], 0.0, 1.0, op0=MAX, op1=MIN)
+                for s in range(SIDES):
+                    cols = slice(s * width, (s + 1) * width)
+                    nc.vector.tensor_scalar(x[:, cols], totals[(r, cb)][:, cols], 0.0, 1.0, op0=MAX, op1=MIN)
             if cb == 0:
                 h1_banks[r] = open_banks(banks1, H1_BANKS, "h1_bank")
             shares = [(SIDES * cb + s, w1_t[s * CB + cb], x[:, s * width : (s + 1) * width]) for s in range(SIDES)]

@@ -21,7 +21,7 @@ H2B = L2 // P
 PER_STEP = H1B // 2
 
 CHUNKS = (128, 128, 128, 128)
-WIDEST = max(CHUNKS)
+SHARED = 2
 BANK = 512
 H1_BANKS = 4
 H2_BANKS = 4
@@ -69,7 +69,7 @@ def tile_nnue_b_kernel(tc, emb, w1, b1, w2, b2, w3, b3, offs, out):
             nc.sync.dma_start(w2_t[kb][:], w2[kb * P : (kb + 1) * P, :])
         nc.sync.dma_start(w3_t[:].rearrange("p (a m) -> p a m", m=M), w3.rearrange("(a p) m -> p a m", p=P))
 
-        zeros = held.tile([P, SIDES * WIDEST], F32, name="zeros")
+        zeros = held.tile([P, SIDES * (CHUNKS[0] + CHUNKS[1])], F32, name="zeros")
         nc.vector.memset(zeros[:], 0.0)
         one = held.tile([P, 1], F32, name="one")
         nc.vector.memset(one[:], 1.0)
@@ -82,17 +82,21 @@ def tile_nnue_b_kernel(tc, emb, w1, b1, w2, b2, w3, b3, offs, out):
         one_less_b2 = held.tile([P, H2B], F32, name="one_less_b2")
         nc.scalar.activation(one_less_b2[:], b2_t[:], IDENTITY, bias=one[:], scale=-1.0)
 
-        def add_slot(total, t0, width, cb, k):
+        def by_side(ap):
+            return ap.rearrange("p (s t) -> p s t", s=SIDES)
+
+        def add_slot(total, t0, cb, k):
+            width = total.shape[2]
             longer = sums.tile([P, SIDES * width], F32, name="longer")
             for s in range(SIDES):
                 first = (k * SIDES * B + s * B + t0) // 16
                 nc.vector.tensor_tensor(
-                    longer[:, s * width : (s + 1) * width],
+                    by_side(longer[:])[:, s, :],
                     emb_t[cb][:].indirect(offsets[:, first : first + width // 16]),
-                    total[:, s * width : (s + 1) * width],
+                    total[:, s, :],
                     ADD,
                 )
-            return longer
+            return by_side(longer[:])
 
         def open_banks(pool, count, name):
             return [pool.tile([P, BANK], F32, name=name) for g in range(count)]
@@ -138,6 +142,7 @@ def tile_nnue_b_kernel(tc, emb, w1, b1, w2, b2, w3, b3, offs, out):
         steps = [(r, cb) for r in range(len(CHUNKS)) for cb in range(CB)]
         starts = [sum(CHUNKS[:r]) for r in range(len(CHUNKS))]
         totals = {}
+        begun = {}
         h1_banks, h2_banks, h1, h2 = {}, {}, {}, {}
 
         def follow(r, part):
@@ -160,12 +165,12 @@ def tile_nnue_b_kernel(tc, emb, w1, b1, w2, b2, w3, b3, offs, out):
             x = xs.tile([P, SIDES * width], BF16, name="x")
             if (r, cb) != steps[-1]:
                 flipped = work.tile([P, BANK], F32, name="flipped")
-                flip(flipped[:, : SIDES * width], totals[(r, cb)][:], one[:])
+                flip(by_side(flipped[:, : SIDES * width]), totals[(r, cb)], one[:])
                 flip(x[:], flipped[:, : SIDES * width], one[:])
             else:
                 for s in range(SIDES):
                     cols = slice(s * width, (s + 1) * width)
-                    nc.vector.tensor_scalar(x[:, cols], totals[(r, cb)][:, cols], 0.0, 1.0, op0=MAX, op1=MIN)
+                    nc.vector.tensor_scalar(x[:, cols], totals[(r, cb)][:, s, :], 0.0, 1.0, op0=MAX, op1=MIN)
             if cb == 0:
                 h1_banks[r] = open_banks(banks1, H1_BANKS, "h1_bank")
             shares = [(SIDES * cb + s, w1_t[s * CB + cb], x[:, s * width : (s + 1) * width]) for s in range(SIDES)]
@@ -178,11 +183,21 @@ def tile_nnue_b_kernel(tc, emb, w1, b1, w2, b2, w3, b3, offs, out):
                 follow(r - 1, cb + 1)
 
         for n, (r, cb) in enumerate(steps):
-            totals[(r, cb)] = zeros
-            for k in range(BAG):
-                totals[(r, cb)] = add_slot(totals[(r, cb)], starts[r], CHUNKS[r], cb, k)
-                if k == 0 and n > 0:
+            if r == 0:
+                total = by_side(zeros[:])
+            elif r == 1:
+                total = begun[cb]
+            else:
+                total = by_side(zeros[:])[:, :, : CHUNKS[r]]
+            slots = range(SHARED, BAG) if r == 1 else range(BAG)
+            for k in slots:
+                if r == 0 and k == SHARED:
+                    begun[cb] = total[:, :, CHUNKS[0] :]
+                    total = total[:, :, : CHUNKS[0]]
+                total = add_slot(total, starts[r], cb, k)
+                if k == slots.start and n > 0:
                     finish_step(*steps[n - 1])
+            totals[(r, cb)] = total
         finish_step(*steps[-1])
         for part in (1, 2):
             follow(len(CHUNKS) - 1, part)

@@ -21,7 +21,7 @@ H2B = L2 // P
 PER_STEP = H1B // 2
 
 CHUNKS = (128, 128, 128, 128)
-SHARED = 2
+SHARED = 1
 BANK = 512
 H1_BANKS = 4
 H2_BANKS = 4
@@ -126,6 +126,17 @@ def tile_nnue_b_kernel(tc, emb, w1, b1, w2, b2, w3, b3, offs, out):
                     flip(flipped[:, cols], bank[:, cols], one_less_b[:, mb : mb + 1])
                 flip(hidden[:, g * used : (g + 1) * used], flipped[:, :used], one[:])
 
+        def clip_on_vector(hidden, banks, blocks, width, b):
+            in_bank = blocks // len(banks)
+            used = in_bank * width
+            for g, bank in enumerate(banks):
+                raised = work.tile([P, BANK], F32, name="raised")
+                for place in range(in_bank):
+                    mb = g * in_bank + place
+                    cols = slice(place * width, (place + 1) * width)
+                    nc.vector.tensor_scalar(raised[:, cols], bank[:, cols], b[:, mb : mb + 1], 0.0, op0=ADD, op1=MAX)
+                nc.vector.tensor_scalar_min(hidden[:, g * used : (g + 1) * used], raised[:, :used], 1.0)
+
         def layer3(t0, width, h2, out_bank):
             for kb in range(H2B):
                 nc.tensor.matmul(
@@ -149,7 +160,10 @@ def tile_nnue_b_kernel(tc, emb, w1, b1, w2, b2, w3, b3, offs, out):
             width = CHUNKS[r]
             if part == 2:
                 h2[r] = acts.tile([P, H2B * width], BF16, name="h2")
-                clip(h2[r], h2_banks[r], H2B, width, one_less_b2)
+                if r < len(CHUNKS) - 1:
+                    clip(h2[r], h2_banks[r], H2B, width, one_less_b2)
+                else:
+                    clip_on_vector(h2[r], h2_banks[r], H2B, width, b2_t)
                 layer3(starts[r], width, h2[r], h2_banks[r][-1][:, BANK - width :])
                 return
             if part == 0:

@@ -18,15 +18,32 @@ CB = C // P
 XB = SIDES * CB
 H1B = L1 // P
 H2B = L2 // P
-PER_STEP = H1B // 2
 
-CHUNKS = (128, 128, 128, 128)
-SHARED = 1
 BANK = 512
-H1_BANKS = 4
-H2_BANKS = 4
+BANKS = 8
+WIDTH = 128
+CHUNKS = B // WIDTH
+WIDE = (0, 1)
+H1_ROWS = (4, 4, 4, 4)
+H2_ROWS = (4, 4)
+LAST_H2_ROWS = (2, 2, 2, 2)
 
 FLOPS = 2 * B * (SIDES * C * L1 + L1 * L2 + L2 * M)
+
+
+def plan_steps():
+    steps = []
+    had = []
+    for r in range(CHUNKS):
+        todo = [cb for cb in range(CB) if cb not in had]
+        had = []
+        for place, cb in enumerate(todo):
+            if r in WIDE and place == 1:
+                steps.append((r, cb, 2, place))
+                had = [cb]
+            else:
+                steps.append((r, cb, 1, place))
+    return steps
 
 
 def tile_nnue_b_kernel(tc, emb, w1, b1, w2, b2, w3, b3, offs, out):
@@ -37,8 +54,7 @@ def tile_nnue_b_kernel(tc, emb, w1, b1, w2, b2, w3, b3, offs, out):
         tc.tile_pool(name="work", bufs=1) as work,
         tc.tile_pool(name="xs", bufs=2 * CB) as xs,
         tc.tile_pool(name="acts", bufs=2) as acts,
-        tc.psum_pool(name="banks1", bufs=H1_BANKS) as banks1,
-        tc.psum_pool(name="banks2", bufs=H2_BANKS) as banks2,
+        tc.psum_pool(name="banks", bufs=BANKS) as banks,
     ):
         offsets = held.tile([P, N // 16], U16, name="offsets")
         nc.sync.dma_start(offsets[:], offs)
@@ -69,7 +85,7 @@ def tile_nnue_b_kernel(tc, emb, w1, b1, w2, b2, w3, b3, offs, out):
             nc.sync.dma_start(w2_t[kb][:], w2[kb * P : (kb + 1) * P, :])
         nc.sync.dma_start(w3_t[:].rearrange("p (a m) -> p a m", m=M), w3.rearrange("(a p) m -> p a m", p=P))
 
-        zeros = held.tile([P, SIDES * (CHUNKS[0] + CHUNKS[1])], F32, name="zeros")
+        zeros = held.tile([P, SIDES * 2 * WIDTH], F32, name="zeros")
         nc.vector.memset(zeros[:], 0.0)
         one = held.tile([P, 1], F32, name="one")
         nc.vector.memset(one[:], 1.0)
@@ -98,120 +114,115 @@ def tile_nnue_b_kernel(tc, emb, w1, b1, w2, b2, w3, b3, offs, out):
                 )
             return by_side(longer[:])
 
-        def open_banks(pool, count, name):
-            return [pool.tile([P, BANK], F32, name=name) for g in range(count)]
+        def open_banks(count):
+            return [banks.tile([P, BANK], F32, name="bank") for g in range(count)]
 
-        def product(banks, blocks, width, shares, last):
-            in_bank = blocks // len(banks)
-            for g, bank in enumerate(banks):
+        def blocks_in(rows, g):
+            return range(sum(rows[:g]), sum(rows[: g + 1]))
+
+        def product(group, rows, shares, last):
+            for g, bank in enumerate(group):
+                here = blocks_in(rows, g)
                 for number, weights, moving in shares:
-                    for place in range(in_bank):
-                        mb = g * in_bank + place
+                    for place, mb in enumerate(here):
                         nc.tensor.matmul(
-                            bank[:, place * width : (place + 1) * width],
+                            bank[:, place * WIDTH : (place + 1) * WIDTH],
                             weights[:, mb * P : (mb + 1) * P],
                             moving,
                             start=(number == 0 and place == 0),
-                            stop=(number == last and place == in_bank - 1),
+                            stop=(number == last and mb == here.stop - 1),
                         )
 
-        def clip(hidden, banks, blocks, width, one_less_b):
-            in_bank = blocks // len(banks)
-            used = in_bank * width
-            for g, bank in enumerate(banks):
+        def clip(hidden, group, rows, one_less_b):
+            for g, bank in enumerate(group):
+                here = blocks_in(rows, g)
                 flipped = work.tile([P, BANK], F32, name="flipped")
-                for place in range(in_bank):
-                    mb = g * in_bank + place
-                    cols = slice(place * width, (place + 1) * width)
+                for place, mb in enumerate(here):
+                    cols = slice(place * WIDTH, (place + 1) * WIDTH)
                     flip(flipped[:, cols], bank[:, cols], one_less_b[:, mb : mb + 1])
-                flip(hidden[:, g * used : (g + 1) * used], flipped[:, :used], one[:])
+                flip(hidden[:, here.start * WIDTH : here.stop * WIDTH], flipped[:, : len(here) * WIDTH], one[:])
 
-        def clip_on_vector(hidden, banks, blocks, width, b):
-            in_bank = blocks // len(banks)
-            used = in_bank * width
-            for g, bank in enumerate(banks):
+        def clip_on_vector(hidden, group, rows, b):
+            for g, bank in enumerate(group):
+                here = blocks_in(rows, g)
                 raised = work.tile([P, BANK], F32, name="raised")
-                for place in range(in_bank):
-                    mb = g * in_bank + place
-                    cols = slice(place * width, (place + 1) * width)
+                for place, mb in enumerate(here):
+                    cols = slice(place * WIDTH, (place + 1) * WIDTH)
                     nc.vector.tensor_scalar(raised[:, cols], bank[:, cols], b[:, mb : mb + 1], 0.0, op0=ADD, op1=MAX)
-                nc.vector.tensor_scalar_min(hidden[:, g * used : (g + 1) * used], raised[:, :used], 1.0)
+                nc.vector.tensor_scalar_min(
+                    hidden[:, here.start * WIDTH : here.stop * WIDTH], raised[:, : len(here) * WIDTH], 1.0
+                )
 
-        def layer3(t0, width, h2, out_bank):
+        steps = plan_steps()
+        totals = {}
+        h1_banks, h2_banks, h1, h2 = {}, {}, {}, {}
+        added = {}
+
+        def layer1(r, cb, x):
+            if r not in h1_banks:
+                h1_banks[r] = open_banks(len(H1_ROWS))
+                added[r] = 0
+            shares = [(added[r] + s, w1_t[s * CB + cb], x[:, s, :]) for s in range(SIDES)]
+            product(h1_banks[r], H1_ROWS, shares, XB - 1)
+            added[r] += SIDES
+
+        def layer2(r, half):
+            rows = H2_ROWS if r < CHUNKS - 1 else LAST_H2_ROWS
+            if half == 0:
+                h2_banks[r] = open_banks(len(rows))
+            shares = [
+                (kb, w2_t[kb], h1[r][:, kb * WIDTH : (kb + 1) * WIDTH])
+                for kb in range(half * H1B // 2, (half + 1) * H1B // 2)
+            ]
+            product(h2_banks[r], rows, shares, H1B - 1)
+
+        def layer3(r):
+            h2[r] = acts.tile([P, H2B * WIDTH], BF16, name="h2")
+            if r < CHUNKS - 1:
+                clip(h2[r], h2_banks[r], H2_ROWS, one_less_b2)
+            else:
+                clip_on_vector(h2[r], h2_banks[r], LAST_H2_ROWS, b2_t)
+            out_bank = open_banks(1)[0][:, :WIDTH]
             for kb in range(H2B):
                 nc.tensor.matmul(
                     out_bank,
                     w3_t[:, kb * M : (kb + 1) * M],
-                    h2[:, kb * width : (kb + 1) * width],
+                    h2[r][:, kb * WIDTH : (kb + 1) * WIDTH],
                     start=(kb == 0),
                     stop=(kb == H2B - 1),
                 )
-            result = work.tile([P, width], F32, name="result")
+            result = work.tile([P, WIDTH], F32, name="result")
             nc.scalar.activation(result[:], out_bank, IDENTITY, bias=b3_t[:], scale=1.0)
-            nc.sync.dma_start(out[:, t0 : t0 + width], result[:])
+            nc.sync.dma_start(out[:, r * WIDTH : (r + 1) * WIDTH], result[:])
 
-        steps = [(r, cb) for r in range(len(CHUNKS)) for cb in range(CB)]
-        starts = [sum(CHUNKS[:r]) for r in range(len(CHUNKS))]
-        totals = {}
-        begun = {}
-        h1_banks, h2_banks, h1, h2 = {}, {}, {}, {}
-
-        def follow(r, part):
-            width = CHUNKS[r]
-            if part == 2:
-                h2[r] = acts.tile([P, H2B * width], BF16, name="h2")
-                if r < len(CHUNKS) - 1:
-                    clip(h2[r], h2_banks[r], H2B, width, one_less_b2)
-                else:
-                    clip_on_vector(h2[r], h2_banks[r], H2B, width, b2_t)
-                layer3(starts[r], width, h2[r], h2_banks[r][-1][:, BANK - width :])
-                return
-            if part == 0:
-                h2_banks[r] = open_banks(banks2, H2_BANKS, "h2_bank")
-            shares = [
-                (kb, w2_t[kb], h1[r][:, kb * width : (kb + 1) * width])
-                for kb in range(part * PER_STEP, (part + 1) * PER_STEP)
-            ]
-            product(h2_banks[r], H2B, width, shares, H1B - 1)
-
-        def finish_step(r, cb):
-            width = CHUNKS[r]
-            x = xs.tile([P, SIDES * width], BF16, name="x")
-            if (r, cb) != steps[-1]:
+        def finish_step(n):
+            r, cb, served, place = steps[n]
+            columns = SIDES * served * WIDTH
+            x = xs.tile([P, columns], BF16, name="x")
+            if n < len(steps) - 1:
                 flipped = work.tile([P, BANK], F32, name="flipped")
-                flip(by_side(flipped[:, : SIDES * width]), totals[(r, cb)], one[:])
-                flip(x[:], flipped[:, : SIDES * width], one[:])
+                flip(by_side(flipped[:, :columns]), totals[n], one[:])
+                flip(x[:], flipped[:, :columns], one[:])
             else:
                 for s in range(SIDES):
-                    cols = slice(s * width, (s + 1) * width)
-                    nc.vector.tensor_scalar(x[:, cols], totals[(r, cb)][:, s, :], 0.0, 1.0, op0=MAX, op1=MIN)
-            if cb == 0:
-                h1_banks[r] = open_banks(banks1, H1_BANKS, "h1_bank")
-            shares = [(SIDES * cb + s, w1_t[s * CB + cb], x[:, s * width : (s + 1) * width]) for s in range(SIDES)]
-            product(h1_banks[r], H1B, width, shares, XB - 1)
-            if cb == CB - 1:
-                h1[r] = acts.tile([P, H1B * width], BF16, name="h1")
-                clip(h1[r], h1_banks[r], H1B, width, one_less_b1)
-                follow(r, 0)
-            if r > 0 and cb < 2:
-                follow(r - 1, cb + 1)
+                    nc.vector.tensor_scalar(by_side(x[:])[:, s, :], totals[n][:, s, :], 0.0, 1.0, op0=MAX, op1=MIN)
+            layer1(r, cb, by_side(x[:])[:, :, :WIDTH])
+            if added[r] == XB:
+                h1[r] = acts.tile([P, H1B * WIDTH], BF16, name="h1")
+                clip(h1[r], h1_banks[r], H1_ROWS, one_less_b1)
+                layer2(r, 0)
+                layer2(r, 1)
+            if r > 0 and place == 0:
+                layer3(r - 1)
+            if served == 2:
+                layer1(r + 1, cb, by_side(x[:])[:, :, WIDTH:])
 
-        for n, (r, cb) in enumerate(steps):
-            if r == 0:
-                total = by_side(zeros[:])
-            elif r == 1:
-                total = begun[cb]
-            else:
-                total = by_side(zeros[:])[:, :, : CHUNKS[r]]
-            slots = range(SHARED, BAG) if r == 1 else range(BAG)
-            for k in slots:
-                if r == 0 and k == SHARED:
-                    begun[cb] = total[:, :, CHUNKS[0] :]
-                    total = total[:, :, : CHUNKS[0]]
-                total = add_slot(total, starts[r], cb, k)
-                if k == slots.start and n > 0:
-                    finish_step(*steps[n - 1])
-            totals[(r, cb)] = total
-        finish_step(*steps[-1])
-        for part in (1, 2):
-            follow(len(CHUNKS) - 1, part)
+        for n, (r, cb, served, place) in enumerate(steps):
+            total = by_side(zeros[:])[:, :, : served * WIDTH]
+            for k in range(BAG):
+                total = add_slot(total, r * WIDTH, cb, k)
+                if k == 0 and n > 0:
+                    finish_step(n - 1)
+            totals[n] = total
+        finish_step(len(steps) - 1)
+        layer3(CHUNKS - 1)

@@ -157,6 +157,7 @@ def tile_nnue_b_kernel(tc, emb, w1, b1, w2, b2, w3, b3, offs, out):
         totals = {}
         h1_banks, h2_banks, h1, h2 = {}, {}, {}, {}
         added = {}
+        early = {}
 
         def layer1(r, cb, x):
             if r not in h1_banks:
@@ -195,18 +196,24 @@ def tile_nnue_b_kernel(tc, emb, w1, b1, w2, b2, w3, b3, offs, out):
             nc.scalar.activation(result[:], out_bank, IDENTITY, bias=b3_t[:], scale=1.0)
             nc.sync.dma_start(out[:, r * WIDTH : (r + 1) * WIDTH], result[:])
 
+        def clipped(total, on_vector):
+            x = xs.tile([P, SIDES * WIDTH], BF16, name="x")
+            if on_vector:
+                for s in range(SIDES):
+                    nc.vector.tensor_scalar(by_side(x[:])[:, s, :], total[:, s, :], 0.0, 1.0, op0=MAX, op1=MIN)
+            else:
+                flipped = work.tile([P, BANK], F32, name="flipped")
+                flip(by_side(flipped[:, : SIDES * WIDTH]), total, one[:])
+                flip(x[:], flipped[:, : SIDES * WIDTH], one[:])
+            return by_side(x[:])
+
         def finish_step(n):
             r, cb, served, place = steps[n]
-            columns = SIDES * served * WIDTH
-            x = xs.tile([P, columns], BF16, name="x")
-            if n < len(steps) - 1:
-                flipped = work.tile([P, BANK], F32, name="flipped")
-                flip(by_side(flipped[:, :columns]), totals[n], one[:])
-                flip(x[:], flipped[:, :columns], one[:])
-            else:
-                for s in range(SIDES):
-                    nc.vector.tensor_scalar(by_side(x[:])[:, s, :], totals[n][:, s, :], 0.0, 1.0, op0=MAX, op1=MIN)
-            layer1(r, cb, by_side(x[:])[:, :, :WIDTH])
+            layer1(r, cb, clipped(totals[n][:, :, :WIDTH], n == len(steps) - 1))
+            if served == 2:
+                early[r + 1] = (cb, totals[n][:, :, WIDTH:])
+            if added[r] == XB - SIDES and r + 1 in early:
+                layer1(r + 1, early[r + 1][0], clipped(early[r + 1][1], False))
             if added[r] == XB:
                 h1[r] = acts.tile([P, H1B * WIDTH], BF16, name="h1")
                 clip(h1[r], h1_banks[r], H1_ROWS, one_less_b1)
@@ -214,8 +221,6 @@ def tile_nnue_b_kernel(tc, emb, w1, b1, w2, b2, w3, b3, offs, out):
                 layer2(r, 1)
             if r > 0 and place == 0:
                 layer3(r - 1)
-            if served == 2:
-                layer1(r + 1, cb, by_side(x[:])[:, :, WIDTH:])
 
         for n, (r, cb, served, place) in enumerate(steps):
             total = by_side(zeros[:])[:, :, : served * WIDTH]

@@ -26,7 +26,7 @@ CHUNKS = B // WIDTH
 WIDE = (0, 1)
 H1_ROWS = (4, 4, 4, 4)
 H2_ROWS = (4, 4)
-LAST_H2_ROWS = (2, 2, 2, 2)
+LAST_H2_ROWS = (2, 2, 2, 1, 1)
 
 FLOPS = 2 * B * (SIDES * C * L1 + L1 * L2 + L2 * M)
 
@@ -133,8 +133,10 @@ def tile_nnue_b_kernel(tc, emb, w1, b1, w2, b2, w3, b3, offs, out):
                             stop=(number == last and mb == here.stop - 1),
                         )
 
-        def clip(hidden, group, rows, one_less_b):
+        def clip(hidden, group, rows, one_less_b, chosen=None):
             for g, bank in enumerate(group):
+                if chosen is not None and g not in chosen:
+                    continue
                 here = blocks_in(rows, g)
                 flipped = work.tile([P, BANK], F32, name="flipped")
                 for place, mb in enumerate(here):
@@ -142,8 +144,10 @@ def tile_nnue_b_kernel(tc, emb, w1, b1, w2, b2, w3, b3, offs, out):
                     flip(flipped[:, cols], bank[:, cols], one_less_b[:, mb : mb + 1])
                 flip(hidden[:, here.start * WIDTH : here.stop * WIDTH], flipped[:, : len(here) * WIDTH], one[:])
 
-        def clip_on_vector(hidden, group, rows, b):
+        def clip_on_vector(hidden, group, rows, b, chosen):
             for g, bank in enumerate(group):
+                if g not in chosen:
+                    continue
                 here = blocks_in(rows, g)
                 raised = work.tile([P, BANK], F32, name="raised")
                 for place, mb in enumerate(here):
@@ -182,7 +186,8 @@ def tile_nnue_b_kernel(tc, emb, w1, b1, w2, b2, w3, b3, offs, out):
             if r < CHUNKS - 1:
                 clip(h2[r], h2_banks[r], H2_ROWS, one_less_b2)
             else:
-                clip_on_vector(h2[r], h2_banks[r], LAST_H2_ROWS, b2_t)
+                clip_on_vector(h2[r], h2_banks[r], LAST_H2_ROWS, b2_t, (0, 2, 4))
+                clip(h2[r], h2_banks[r], LAST_H2_ROWS, one_less_b2, (1, 3))
             out_bank = open_banks(1)[0][:, :WIDTH]
             for kb in range(H2B):
                 nc.tensor.matmul(

@@ -67,11 +67,11 @@ def tile_nnue_b_kernel(tc, emb, w1, b1, w2, b2, w3, b3, offs, out):
         b2_t = held.tile([P, H2B], F32, name="b2_t")
         b3_t = held.tile([P, 1], F32, name="b3_t")
 
-        def load_emb(cb):
-            nc.sync.dma_start(emb_t[cb][:], emb[cb * P : (cb + 1) * P, :])
+        def load_emb(cb, queue):
+            queue.dma_start(emb_t[cb][:], emb[cb * P : (cb + 1) * P, :])
 
-        load_emb(0)
-        load_emb(1)
+        load_emb(0, nc.scalar)
+        load_emb(1, nc.sync)
         nc.sync.dma_start(b1_t[:], b1.rearrange("(a p) o -> p (a o)", p=P))
         nc.sync.dma_start(b2_t[:], b2.rearrange("(a p) o -> p (a o)", p=P))
         nc.sync.dma_start(b3_t[:], b3)
@@ -80,7 +80,7 @@ def tile_nnue_b_kernel(tc, emb, w1, b1, w2, b2, w3, b3, offs, out):
                 kb = s * CB + cb
                 nc.sync.dma_start(w1_t[kb][:], w1[kb * P : (kb + 1) * P, :])
             if cb + 2 < CB:
-                load_emb(cb + 2)
+                load_emb(cb + 2, nc.sync)
         for kb in range(H1B):
             nc.sync.dma_start(w2_t[kb][:], w2[kb * P : (kb + 1) * P, :])
         nc.sync.dma_start(w3_t[:].rearrange("p (a m) -> p a m", m=M), w3.rearrange("(a p) m -> p a m", p=P))

import concourse.mybir as mybir

F32 = mybir.dt.float32
BF16 = mybir.dt.bfloat16
U16 = mybir.dt.uint16
ADD = mybir.AluOpType.add
MAX = mybir.AluOpType.max
MIN = mybir.AluOpType.min
RELU = mybir.ActivationFunctionType.Relu
IDENTITY = mybir.ActivationFunctionType.Identity

P = 128
C, S, B, BAG, SIDES = 512, 2048, 512, 8, 2
L1, L2, M = 2048, 1024, 128
N = BAG * SIDES * B

CB = C // P
XB = SIDES * CB
H1B = L1 // P
H2B = L2 // P

BANK = 512
BANKS = 8
WIDTH = 128
CHUNKS = B // WIDTH
WIDE = (0, 1)
H1_ROWS = (4, 4, 4, 4)
H2_ROWS = (4, 4)
LAST_H2_ROWS = (2, 2, 2, 1, 1)

FLOPS = 2 * B * (SIDES * C * L1 + L1 * L2 + L2 * M)


def plan_steps():
    steps = []
    had = []
    for r in range(CHUNKS):
        todo = [cb for cb in range(CB) if cb not in had]
        had = []
        for place, cb in enumerate(todo):
            if r in WIDE and place == 1:
                steps.append((r, cb, 2, place))
                had = [cb]
            else:
                steps.append((r, cb, 1, place))
    return steps


def tile_nnue_b_kernel(tc, emb, w1, b1, w2, b2, w3, b3, offs, out):
    nc = tc.nc
    with (
        tc.tile_pool(name="held", bufs=1) as held,
        tc.tile_pool(name="sums", bufs=3 * BAG) as sums,
        tc.tile_pool(name="work", bufs=1) as work,
        tc.tile_pool(name="xs", bufs=2 * CB) as xs,
        tc.tile_pool(name="acts", bufs=2) as acts,
        tc.psum_pool(name="banks", bufs=BANKS) as banks,
    ):
        offsets = held.tile([P, N // 16], U16, name="offsets")
        nc.sync.dma_start(offsets[:], offs)

        emb_t = [held.tile([P, S], F32, name=f"emb{cb}") for cb in range(CB)]
        w1_t = [held.tile([P, L1], BF16, name=f"w1_{kb}") for kb in range(XB)]
        w2_t = [held.tile([P, L2], BF16, name=f"w2_{kb}") for kb in range(H1B)]
        w3_t = held.tile([P, H2B * M], BF16, name="w3_t")
        b1_t = held.tile([P, H1B], F32, name="b1_t")
        b2_t = held.tile([P, H2B], F32, name="b2_t")
        b3_t = held.tile([P, 1], F32, name="b3_t")

        def load_emb(cb, queue):
            queue.dma_start(emb_t[cb][:], emb[cb * P : (cb + 1) * P, :])

        load_emb(0, nc.scalar)
        load_emb(1, nc.sync)
        nc.sync.dma_start(b1_t[:], b1.rearrange("(a p) o -> p (a o)", p=P))
        nc.sync.dma_start(b2_t[:], b2.rearrange("(a p) o -> p (a o)", p=P))
        nc.sync.dma_start(b3_t[:], b3)
        for cb in range(CB):
            for s in range(SIDES):
                kb = s * CB + cb
                nc.sync.dma_start(w1_t[kb][:], w1[kb * P : (kb + 1) * P, :])
            if cb + 2 < CB:
                load_emb(cb + 2, nc.sync)
        for kb in range(H1B):
            nc.sync.dma_start(w2_t[kb][:], w2[kb * P : (kb + 1) * P, :])
        nc.sync.dma_start(w3_t[:].rearrange("p (a m) -> p a m", m=M), w3.rearrange("(a p) m -> p a m", p=P))

        zeros = held.tile([P, SIDES * 2 * WIDTH], F32, name="zeros")
        nc.vector.memset(zeros[:], 0.0)
        one = held.tile([P, 1], F32, name="one")
        nc.vector.memset(one[:], 1.0)

        def flip(out_ap, in_ap, bias_ap):
            nc.scalar.activation(out_ap, in_ap, RELU, bias=bias_ap, scale=-1.0)

        one_less_b1 = held.tile([P, H1B], F32, name="one_less_b1")
        nc.scalar.activation(one_less_b1[:], b1_t[:], IDENTITY, bias=one[:], scale=-1.0)
        one_less_b2 = held.tile([P, H2B], F32, name="one_less_b2")
        nc.scalar.activation(one_less_b2[:], b2_t[:], IDENTITY, bias=one[:], scale=-1.0)

        def by_side(ap):
            return ap.rearrange("p (s t) -> p s t", s=SIDES)

        def add_slot(total, t0, cb, k):
            width = total.shape[2]
            longer = sums.tile([P, SIDES * width], F32, name="longer")
            for s in range(SIDES):
                first = (k * SIDES * B + s * B + t0) // 16
                nc.vector.tensor_tensor(
                    by_side(longer[:])[:, s, :],
                    emb_t[cb][:].indirect(offsets[:, first : first + width // 16]),
                    total[:, s, :],
                    ADD,
                )
            return by_side(longer[:])

        def open_banks(count):
            return [banks.tile([P, BANK], F32, name="bank") for g in range(count)]

        def blocks_in(rows, g):
            return range(sum(rows[:g]), sum(rows[: g + 1]))

        def product(group, rows, shares, last):
            for g, bank in enumerate(group):
                here = blocks_in(rows, g)
                for number, weights, moving in shares:
                    for place, mb in enumerate(here):
                        nc.tensor.matmul(
                            bank[:, place * WIDTH : (place + 1) * WIDTH],
                            weights[:, mb * P : (mb + 1) * P],
                            moving,
                            start=(number == 0 and place == 0),
                            stop=(number == last and mb == here.stop - 1),
                        )

        def clip(hidden, group, rows, one_less_b, chosen=None):
            for g, bank in enumerate(group):
                if chosen is not None and g not in chosen:
                    continue
                here = blocks_in(rows, g)
                flipped = work.tile([P, BANK], F32, name="flipped")
                for place, mb in enumerate(here):
                    cols = slice(place * WIDTH, (place + 1) * WIDTH)
                    flip(flipped[:, cols], bank[:, cols], one_less_b[:, mb : mb + 1])
                flip(hidden[:, here.start * WIDTH : here.stop * WIDTH], flipped[:, : len(here) * WIDTH], one[:])

        def clip_on_vector(hidden, group, rows, b, chosen):
            for g, bank in enumerate(group):
                if g not in chosen:
                    continue
                here = blocks_in(rows, g)
                raised = work.tile([P, BANK], F32, name="raised")
                for place, mb in enumerate(here):
                    cols = slice(place * WIDTH, (place + 1) * WIDTH)
                    nc.vector.tensor_scalar(raised[:, cols], bank[:, cols], b[:, mb : mb + 1], 0.0, op0=ADD, op1=MAX)
                nc.vector.tensor_scalar_min(
                    hidden[:, here.start * WIDTH : here.stop * WIDTH], raised[:, : len(here) * WIDTH], 1.0
                )

        steps = plan_steps()
        totals = {}
        h1_banks, h2_banks, h1, h2 = {}, {}, {}, {}
        added = {}
        early = {}

        def layer1(r, cb, x):
            if r not in h1_banks:
                h1_banks[r] = open_banks(len(H1_ROWS))
                added[r] = 0
            shares = [(added[r] + s, w1_t[s * CB + cb], x[:, s, :]) for s in range(SIDES)]
            product(h1_banks[r], H1_ROWS, shares, XB - 1)
            added[r] += SIDES

        def layer2(r, half):
            rows = H2_ROWS if r < CHUNKS - 1 else LAST_H2_ROWS
            if half == 0:
                h2_banks[r] = open_banks(len(rows))
            shares = [
                (kb, w2_t[kb], h1[r][:, kb * WIDTH : (kb + 1) * WIDTH])
                for kb in range(half * H1B // 2, (half + 1) * H1B // 2)
            ]
            product(h2_banks[r], rows, shares, H1B - 1)

        def layer3(r):
            h2[r] = acts.tile([P, H2B * WIDTH], BF16, name="h2")
            if r < CHUNKS - 1:
                clip(h2[r], h2_banks[r], H2_ROWS, one_less_b2)
            else:
                clip_on_vector(h2[r], h2_banks[r], LAST_H2_ROWS, b2_t, (0, 2, 4))
                clip(h2[r], h2_banks[r], LAST_H2_ROWS, one_less_b2, (1, 3))
            out_bank = open_banks(1)[0][:, :WIDTH]
            for kb in range(H2B):
                nc.tensor.matmul(
                    out_bank,
                    w3_t[:, kb * M : (kb + 1) * M],
                    h2[r][:, kb * WIDTH : (kb + 1) * WIDTH],
                    start=(kb == 0),
                    stop=(kb == H2B - 1),
                )
            result = work.tile([P, WIDTH], F32, name="result")
            nc.scalar.activation(result[:], out_bank, IDENTITY, bias=b3_t[:], scale=1.0)
            nc.sync.dma_start(out[:, r * WIDTH : (r + 1) * WIDTH], result[:])

        def clipped(total, on_vector):
            x = xs.tile([P, SIDES * WIDTH], BF16, name="x")
            if on_vector:
                for s in range(SIDES):
                    nc.vector.tensor_scalar(by_side(x[:])[:, s, :], total[:, s, :], 0.0, 1.0, op0=MAX, op1=MIN)
            else:
                flipped = work.tile([P, BANK], F32, name="flipped")
                flip(by_side(flipped[:, : SIDES * WIDTH]), total, one[:])
                flip(x[:], flipped[:, : SIDES * WIDTH], one[:])
            return by_side(x[:])

        def finish_step(n):
            r, cb, served, place = steps[n]
            layer1(r, cb, clipped(totals[n][:, :, :WIDTH], n == len(steps) - 1))
            if served == 2:
                early[r + 1] = (cb, totals[n][:, :, WIDTH:])
            if added[r] == XB - SIDES and r + 1 in early:
                layer1(r + 1, early[r + 1][0], clipped(early[r + 1][1], False))
            if added[r] == XB:
                h1[r] = acts.tile([P, H1B * WIDTH], BF16, name="h1")
                clip(h1[r], h1_banks[r], H1_ROWS, one_less_b1)
                layer2(r, 0)
                layer2(r, 1)
            if r > 0 and place == 0:
                layer3(r - 1)

        for n, (r, cb, served, place) in enumerate(steps):
            total = by_side(zeros[:])[:, :, : served * WIDTH]
            for k in range(BAG):
                total = add_slot(total, r * WIDTH, cb, k)
                if k == 0 and n > 0:
                    finish_step(n - 1)
            totals[n] = total
        finish_step(len(steps) - 1)
        layer3(CHUNKS - 1)
